import numpy as np
import ml_dtypes


def mxq(x, axis, fmt="e4m3"):
    dtype, down = {"e4m3": (ml_dtypes.float8_e4m3fn, 7), "e5m2": (ml_dtypes.float8_e5m2, 14)}[fmt]
    v = np.moveaxis(np.asarray(x, np.float32).astype(ml_dtypes.bfloat16).astype(np.float64), axis, -1)
    blocks = v.reshape(v.shape[:-1] + (-1, 32))
    amax = np.abs(blocks).max(-1, keepdims=True)
    byte = np.maximum(np.where(amax > 0, np.frexp(amax)[1] - 1 + 127, 0) - down, 1)
    scale = np.exp2(byte - 127.0)
    codes = (blocks / scale).astype(np.float32).astype(dtype).astype(np.float64)
    return np.moveaxis((codes * scale).reshape(v.shape), -1, axis)


WIDE = False


def mx_kscale(k):
    if not WIDE:
        return np.ones(k)
    levels = np.array([10, -10, 5, -5, 0])
    a = np.random.permutation(np.resize(levels, k // 512 * 4)).reshape(k // 512, 4)
    idx = np.arange(k)
    return np.exp2(a[idx // 512, idx % 128 // 32])


BF16 = ml_dtypes.bfloat16


def bf(x):
    return np.asarray(x, np.float32).astype(BF16)


def f64(x):
    return np.asarray(x).astype(np.float64)


B, N, E, L, A, H1, H2, G = 1024, 8, 8, 384, 128, 512, 1024, 8
D = L + A
EPS = 1e-5


def mish(v):
    return v * np.tanh(np.log(1.0 + np.exp(v)))


def layer_norm(v, gamma, beta):
    mu = v.mean(-1, keepdims=True)
    var = v.var(-1, keepdims=True)
    return (v - mu) / np.sqrt(var + EPS) * gamma + beta


def setup_inputs():
    s = mx_kscale(D)
    r = np.random.standard_normal
    return {"tokens": bf(r((B, N, D)) * s),
            "logits": bf(r((B, N, E))),
            "W1": bf(r((E, D, H1)) / np.sqrt(D) / s[:, None]),
            "b1": bf(0.1 * r((E, H1))),
            "g1": bf(1.0 + 0.1 * r((E, H1))),
            "be1": bf(0.1 * r((E, H1)))}


def reference(tokens, logits, W1, b1, g1, be1):
    tok, lg = f64(tokens), f64(logits)
    ex = np.exp(lg - lg.max(1, keepdims=True))
    disp = ex / ex.sum(1, keepdims=True)
    slot = sum(disp[:, n, :].T[:, :, None] * tok[None, :, n, :] for n in range(N))
    h = (mxq(slot, 2, "e4m3") @ mxq(f64(W1), 1, "e4m3")) + f64(b1)[:, None, :]
    h = mish(layer_norm(h, f64(g1)[:, None, :], f64(be1)[:, None, :]))
    return h.transpose(1, 0, 2)

@@ -1,0 +1,250 @@
+from contextlib import ExitStack
+
+import concourse.mybir as mybir
+from concourse.masks import make_identity
+
+F32 = mybir.dt.float32
+BF16 = mybir.dt.bfloat16
+U32 = mybir.dt.uint32
+U8 = mybir.dt.uint8
+FP8X4 = mybir.dt.float8_e4m3fn_x4
+ALU = mybir.AluOpType
+ACT = mybir.ActivationFunctionType
+AX = mybir.AxisListType
+
+P = 128
+B, NA, E, DK, H = 1024, 8, 8, 512, 512
+NBT = B // P
+PACK = 4
+GB = 16
+NG = P // GB
+EPS = 1e-5
+FLOPS = 2 * B * E * DK * H + 2 * B * E * NA * DK
+
+BD_TILES = (1, 3, 5)
+ORDER = (0, 1, 2, 3, 4, 5, 6, 7)
+
+
+def tile_softmoedynamics_pa_t_kernel(tc, tokens, logits, W1, b1, g1, be1, out):
+    nc = tc.nc
+    with ExitStack() as ctx:
+        const = ctx.enter_context(tc.tile_pool(name="const", bufs=1))
+        wstage = ctx.enter_context(tc.tile_pool(name="wstage", bufs=2))
+        tokp = ctx.enter_context(tc.tile_pool(name="tokp", bufs=2))
+        castp = ctx.enter_context(tc.tile_pool(name="castp", bufs=3))
+        bdp = ctx.enter_context(tc.tile_pool(name="bdp", bufs=1))
+        prodp = ctx.enter_context(tc.tile_pool(name="prodp", bufs=2))
+        grpp = ctx.enter_context(tc.tile_pool(name="grpp", bufs=1))
+        codep = ctx.enter_context(tc.tile_pool(name="codep", bufs=2))
+        xp = ctx.enter_context(tc.tile_pool(name="xp", bufs=1))
+        tvp = ctx.enter_context(tc.tile_pool(name="tvp", bufs=2))
+        up = ctx.enter_context(tc.tile_pool(name="up", bufs=2))
+        junkp = ctx.enter_context(tc.tile_pool(name="junkp", bufs=2))
+        statp = ctx.enter_context(tc.tile_pool(name="statp", bufs=2))
+        ps_bd = ctx.enter_context(tc.psum_pool(name="ps_bd", bufs=1))
+        ps_slot = ctx.enter_context(tc.psum_pool(name="ps_slot", bufs=4))
+        ps_h = ctx.enter_context(tc.psum_pool(name="ps_h", bufs=3))
+
+        lg = const.tile([P, NBT, NA, E], BF16)
+        nc.sync.dma_start(out=lg[:], in_=logits.rearrange("(t p) n e -> p t n e", p=P))
+
+        ident = const.tile([P, P], F32)
+        make_identity(nc, ident[:])
+        mask16 = const.tile([P, GB], F32)
+        nc.vector.tensor_reduce(
+            out=mask16[:], in_=ident[:].rearrange("p (g c) -> p c g", c=GB), axis=AX.X, op=ALU.add
+        )
+        neghalf = const.tile([P, E], F32)
+        nc.vector.memset(neghalf[:], -0.5)
+
+        b1b = const.tile([P, E * H], BF16)
+        g1b = const.tile([P, E * H], BF16)
+        be1b = const.tile([P, E * H], BF16)
+        nc.scalar.dma_start(out=b1b[:], in_=b1.rearrange("e h -> (e h)").partition_broadcast(P))
+        nc.scalar.dma_start(out=g1b[:], in_=g1.rearrange("e h -> (e h)").partition_broadcast(P))
+        nc.scalar.dma_start(out=be1b[:], in_=be1.rearrange("e h -> (e h)").partition_broadcast(P))
+
+        full = [P, NBT, NA, E]
+        mx = const.tile([P, NBT, E], F32)
+        nc.vector.tensor_reduce(out=mx[:], in_=lg[:].rearrange("p t n e -> p t e n"), axis=AX.X, op=ALU.max)
+        ex = const.tile(full, F32)
+        nc.vector.tensor_tensor(out=ex[:], in0=lg[:], in1=mx[:].unsqueeze(2).to_broadcast(full), op=ALU.subtract)
+        exf = ex[:].rearrange("p t n e -> p (t n e)")
+        nc.scalar.activation(out=exf, in_=exf, func=ACT.Exp)
+        den = const.tile([P, NBT, E], F32)
+        nc.vector.tensor_reduce(out=den[:], in_=ex[:].rearrange("p t n e -> p t e n"), axis=AX.X, op=ALU.add)
+        rden = const.tile([P, NBT, E], F32)
+        nc.vector.reciprocal(out=rden[:], in_=den[:])
+        disp = const.tile(full, F32)
+        nc.vector.tensor_tensor(out=disp[:], in0=ex[:], in1=rden[:].unsqueeze(2).to_broadcast(full), op=ALU.mult)
+
+        wcodes = const.tile([P, E, H], U32, align_bytes=64)
+        wscales = const.tile([P, E, H], U8, align_bytes=64)
+
+        def quantise_w(e):
+            wraw = wstage.tile([P, PACK, H], BF16)
+            nc.sync.dma_start(out=wraw[:], in_=W1[e].rearrange("(t p) h -> p t h", p=P))
+            wgrp = wstage.tile([P, H, PACK], BF16, align_bytes=64)
+            dst = wgrp[:].rearrange("p (c i) t -> p c t i", i=4)
+            src = wraw[:].rearrange("p t (c i) -> p c t i", i=4)
+            if e % 2 == 0:
+                nc.scalar.copy(out=dst, in_=src)
+            else:
+                nc.vector.tensor_copy(out=dst, in_=src)
+            nc.vector.quantize_mx(
+                out=wcodes[:, e, :].bitcast(FP8X4),
+                scales=wscales[:, e, :],
+                in_=wgrp[:].rearrange("p h t -> p (h t)"),
+            )
+
+        def slot_block_diagonal(bt, grouped):
+            tok = tokp.tile([P, NG, DK], BF16, tag="tok")
+            nc.sync.dma_start(
+                out=tok[:], in_=tokens[bt * P : (bt + 1) * P].rearrange("(g b) n d -> (b n) g d", g=NG)
+            )
+            shape = [P, E, GB, NA]
+            yexp = bdp.tile(shape, F32)
+            nc.vector.tensor_tensor(
+                out=yexp[:],
+                in0=disp[:, bt].rearrange("p n e -> p e n").unsqueeze(2).to_broadcast(shape),
+                in1=mask16[:].unsqueeze(1).unsqueeze(3).to_broadcast(shape),
+                op=ALU.mult,
+            )
+            bd = bdp.tile([P, NG, E, GB], F32)
+            for half in range(2):
+                pbd = ps_bd.tile([P, 4, P], F32)
+                for j in range(4):
+                    nc.tensor.transpose(
+                        pbd[:, j, :], yexp[:, half * 4 + j].rearrange("p c n -> p (c n)"), ident[:]
+                    )
+                nc.vector.tensor_copy(
+                    out=bd[:, :, half * 4 : (half + 1) * 4, :],
+                    in_=pbd[:].rearrange("p e (g c) -> p g e c", c=GB),
+                )
+            for g in range(NG):
+                tokf = castp.tile([P, DK], F32)
+                nc.scalar.copy(out=tokf[:], in_=tok[:, g, :])
+                pslot = ps_slot.tile([P, PACK, P], F32, tag="pslot")
+                for t in range(PACK):
+                    nc.tensor.matmul(
+                        pslot[:, t, :],
+                        lhsT=tokf[:, t * P : (t + 1) * P],
+                        rhs=bd[:, g].rearrange("p e c -> p (e c)"),
+                        start=True,
+                        stop=True,
+                    )
+                nc.scalar.copy(
+                    out=grouped[:, :, g * GB : (g + 1) * GB, :],
+                    in_=pslot[:].rearrange("p t (e c) -> p e c t", c=GB),
+                )
+
+        def slot_products(bt, grouped):
+            tok = tokp.tile([P, NA, DK], BF16, tag="tok")
+            nc.sync.dma_start(out=tok[:], in_=tokens[bt * P : (bt + 1) * P])
+            for e in range(E):
+                prod = prodp.tile([P, NA, DK], F32)
+                for n in range(NA):
+                    nc.vector.tensor_scalar(
+                        out=prod[:, n, :],
+                        in0=tok[:, n, :],
+                        scalar1=disp[:, bt, n, e : e + 1],
+                        scalar2=None,
+                        op0=ALU.mult,
+                    )
+                pslot = ps_slot.tile([P, PACK, P], F32, tag="pslot")
+                for t in range(PACK):
+                    for n in range(NA):
+                        nc.tensor.matmul(
+                            pslot[:, t, :],
+                            lhsT=prod[:, n, t * P : (t + 1) * P],
+                            rhs=ident[:],
+                            is_transpose=True,
+                            start=(n == 0),
+                            stop=(n == NA - 1),
+                        )
+                nc.scalar.copy(out=grouped[:, e], in_=pslot[:].rearrange("p t b -> p b t"))
+
+        def expert_layer(bt, grouped):
+            scodes = codep.tile([P, E * P], U32, align_bytes=64)
+            sscales = codep.tile([P, E * P], U8, align_bytes=64)
+            nc.vector.quantize_mx(
+                out=scodes[:].bitcast(FP8X4),
+                scales=sscales[:],
+                in_=grouped[:].rearrange("p e b t -> p (e b t)"),
+            )
+            x = xp.tile([P, E, H], F32)
+            tv = tvp.tile([P, E, H], F32)
+            u = up.tile([P, E * H], F32)
+            sx = statp.tile([P, E], F32)
+            negmu = statp.tile([P, E], F32)
+            ssq = statp.tile([P, E], F32)
+            vareps = statp.tile([P, E], F32)
+            rstd = statp.tile([P, E], F32)
+            for e in range(E):
+                ph = ps_h.tile([P, H], F32)
+                nc.tensor.matmul_mx(
+                    out=ph[:],
+                    lhsT=scodes[:, e * P : (e + 1) * P].bitcast(FP8X4),
+                    lhsT_scale=sscales[:, e * P : (e + 1) * P],
+                    rhs=wcodes[:, e, :].bitcast(FP8X4),
+                    rhs_scale=wscales[:, e, :],
+                    start=True,
+                    stop=True,
+                )
+                nc.vector.scalar_tensor_tensor(
+                    out=x[:, e, :],
+                    in0=ph[:],
+                    scalar=1.0,
+                    in1=b1b[:, e * H : (e + 1) * H],
+                    op0=ALU.mult,
+                    op1=ALU.add,
+                    accum_out=sx[:, e : e + 1],
+                )
+            nc.vector.tensor_scalar(out=negmu[:], in0=sx[:], scalar1=-1.0 / H, scalar2=None, op0=ALU.mult)
+            for e in range(E):
+                junk = junkp.tile([P, H], BF16)
+                nc.scalar.activation(
+                    out=junk[:],
+                    in_=x[:, e, :],
+                    func=ACT.Square,
+                    bias=negmu[:, e : e + 1],
+                    scale=1.0,
+                    accum_out=ssq[:, e : e + 1],
+                )
+                nc.vector.scalar_tensor_tensor(
+                    out=tv[:, e, :],
+                    in0=x[:, e, :],
+                    scalar=negmu[:, e : e + 1],
+                    in1=g1b[:, e * H : (e + 1) * H],
+                    op0=ALU.add,
+                    op1=ALU.mult,
+                )
+            nc.vector.tensor_scalar(
+                out=vareps[:], in0=ssq[:], scalar1=1.0 / H, scalar2=EPS, op0=ALU.mult, op1=ALU.add
+            )
+            nc.gpsimd.tensor_tensor(out=rstd[:], in0=vareps[:], in1=neghalf[:], op=ALU.pow)
+            for e in range(E):
+                nc.vector.scalar_tensor_tensor(
+                    out=tv[:, e, :],
+                    in0=tv[:, e, :],
+                    scalar=rstd[:, e : e + 1],
+                    in1=be1b[:, e * H : (e + 1) * H],
+                    op0=ALU.mult,
+                    op1=ALU.add,
+                )
+            tvf = tv[:].rearrange("p e h -> p (e h)")
+            nc.scalar.activation(out=u[:], in_=tvf, func=ACT.Exp)
+            nc.scalar.activation(out=u[:], in_=u[:], func=ACT.Ln, bias=1.0, scale=1.0)
+            nc.scalar.activation(out=u[:], in_=u[:], func=ACT.Tanh)
+            nc.vector.tensor_tensor(out=u[:], in0=tvf, in1=u[:], op=ALU.mult)
+            nc.sync.dma_start(out=out[bt * P : (bt + 1) * P].rearrange("b e h -> b (e h)"), in_=u[:])
+
+        for e in range(E):
+            quantise_w(e)
+        for bt in ORDER:
+            grouped = grpp.tile([P, E, P, PACK], BF16, align_bytes=64)
+            if bt in BD_TILES:
+                slot_block_diagonal(bt, grouped)
+            else:
+                slot_products(bt, grouped)
+            expert_layer(bt, grouped)

@@ -21,24 +21,27 @@ NG = P // GB
 EPS = 1e-5
 FLOPS = 2 * B * E * DK * H + 2 * B * E * NA * DK
 
-BD_TILES = (1, 3, 5)
-ORDER = (0, 1, 2, 3, 4, 5, 6, 7)
+KINDS = "DPDPDPPP"
+MODES = ((2, 2), (4, 2), (4, 2), (8, 2), (8, 2))
+W_ON_VECTOR = (1, 3, 5, 7)
+PROLOGUE = ("W0", "d", "d", "p", "W1", "d", "d", "p", "W2", "d", "d", "p", "W3", "d", "d", "p", "W4", "p", "W5", "p", "W6", "p", "W7", "p")
+PERIOD = ("E", "E", "S1", "p", "ST", "d", "F", "d", "F", "p", "D", "G", "d", "G", "p", "H", "p", "d", "p")
+PIECES = 2
 
 
 def tile_softmoedynamics_pa_t_kernel(tc, tokens, logits, W1, b1, g1, be1, out):
     nc = tc.nc
     with ExitStack() as ctx:
         const = ctx.enter_context(tc.tile_pool(name="const", bufs=1))
-        wstage = ctx.enter_context(tc.tile_pool(name="wstage", bufs=2))
         tokp = ctx.enter_context(tc.tile_pool(name="tokp", bufs=2))
+        tokd = ctx.enter_context(tc.tile_pool(name="tokd", bufs=4))
         castp = ctx.enter_context(tc.tile_pool(name="castp", bufs=3))
         bdp = ctx.enter_context(tc.tile_pool(name="bdp", bufs=1))
         prodp = ctx.enter_context(tc.tile_pool(name="prodp", bufs=2))
         grpp = ctx.enter_context(tc.tile_pool(name="grpp", bufs=1))
-        codep = ctx.enter_context(tc.tile_pool(name="codep", bufs=2))
+        codep = ctx.enter_context(tc.tile_pool(name="codep", bufs=3))
         xp = ctx.enter_context(tc.tile_pool(name="xp", bufs=1))
         tvp = ctx.enter_context(tc.tile_pool(name="tvp", bufs=2))
-        up = ctx.enter_context(tc.tile_pool(name="up", bufs=2))
         junkp = ctx.enter_context(tc.tile_pool(name="junkp", bufs=2))
         statp = ctx.enter_context(tc.tile_pool(name="statp", bufs=2))
         ps_bd = ctx.enter_context(tc.psum_pool(name="ps_bd", bufs=1))
@@ -81,90 +84,29 @@ def tile_softmoedynamics_pa_t_kernel(tc, tokens, logits, W1, b1, g1, be1, out):
         wcodes = const.tile([P, E, H], U32, align_bytes=64)
         wscales = const.tile([P, E, H], U8, align_bytes=64)
 
-        def quantise_w(e):
+        def quantise_w(e, wstage):
             wraw = wstage.tile([P, PACK, H], BF16)
             nc.sync.dma_start(out=wraw[:], in_=W1[e].rearrange("(t p) h -> p t h", p=P))
             wgrp = wstage.tile([P, H, PACK], BF16, align_bytes=64)
             dst = wgrp[:].rearrange("p (c i) t -> p c t i", i=4)
             src = wraw[:].rearrange("p t (c i) -> p c t i", i=4)
-            if e % 2 == 0:
-                nc.scalar.copy(out=dst, in_=src)
-            else:
+            if e in W_ON_VECTOR:
                 nc.vector.tensor_copy(out=dst, in_=src)
+            else:
+                nc.scalar.copy(out=dst, in_=src)
             nc.vector.quantize_mx(
                 out=wcodes[:, e, :].bitcast(FP8X4),
                 scales=wscales[:, e, :],
                 in_=wgrp[:].rearrange("p h t -> p (h t)"),
             )
 
-        def slot_block_diagonal(bt, grouped):
-            tok = tokp.tile([P, NG, DK], BF16, tag="tok")
-            nc.sync.dma_start(
-                out=tok[:], in_=tokens[bt * P : (bt + 1) * P].rearrange("(g b) n d -> (b n) g d", g=NG)
-            )
-            shape = [P, E, GB, NA]
-            yexp = bdp.tile(shape, F32)
-            nc.vector.tensor_tensor(
-                out=yexp[:],
-                in0=disp[:, bt].rearrange("p n e -> p e n").unsqueeze(2).to_broadcast(shape),
-                in1=mask16[:].unsqueeze(1).unsqueeze(3).to_broadcast(shape),
-                op=ALU.mult,
-            )
-            bd = bdp.tile([P, NG, E, GB], F32)
-            for half in range(2):
-                pbd = ps_bd.tile([P, 4, P], F32)
-                for j in range(4):
-                    nc.tensor.transpose(
-                        pbd[:, j, :], yexp[:, half * 4 + j].rearrange("p c n -> p (c n)"), ident[:]
-                    )
-                nc.vector.tensor_copy(
-                    out=bd[:, :, half * 4 : (half + 1) * 4, :],
-                    in_=pbd[:].rearrange("p e (g c) -> p g e c", c=GB),
-                )
-            for g in range(NG):
-                tokf = castp.tile([P, DK], F32)
-                nc.scalar.copy(out=tokf[:], in_=tok[:, g, :])
-                pslot = ps_slot.tile([P, PACK, P], F32, tag="pslot")
-                for t in range(PACK):
-                    nc.tensor.matmul(
-                        pslot[:, t, :],
-                        lhsT=tokf[:, t * P : (t + 1) * P],
-                        rhs=bd[:, g].rearrange("p e c -> p (e c)"),
-                        start=True,
-                        stop=True,
-                    )
-                nc.scalar.copy(
-                    out=grouped[:, :, g * GB : (g + 1) * GB, :],
-                    in_=pslot[:].rearrange("p t (e c) -> p e c t", c=GB),
-                )
+        p_tiles = [bt for bt in range(NBT) if KINDS[bt] == "P"]
+        d_tiles = [bt for bt in range(NBT) if KINDS[bt] == "D"]
+        state = {"p": 0, "d": 0}
+        live = {}
+        codes = {}
 
-        def slot_products(bt, grouped):
-            tok = tokp.tile([P, NA, DK], BF16, tag="tok")
-            nc.sync.dma_start(out=tok[:], in_=tokens[bt * P : (bt + 1) * P])
-            for e in range(E):
-                prod = prodp.tile([P, NA, DK], F32)
-                for n in range(NA):
-                    nc.vector.tensor_scalar(
-                        out=prod[:, n, :],
-                        in0=tok[:, n, :],
-                        scalar1=disp[:, bt, n, e : e + 1],
-                        scalar2=None,
-                        op0=ALU.mult,
-                    )
-                pslot = ps_slot.tile([P, PACK, P], F32, tag="pslot")
-                for t in range(PACK):
-                    for n in range(NA):
-                        nc.tensor.matmul(
-                            pslot[:, t, :],
-                            lhsT=prod[:, n, t * P : (t + 1) * P],
-                            rhs=ident[:],
-                            is_transpose=True,
-                            start=(n == 0),
-                            stop=(n == NA - 1),
-                        )
-                nc.scalar.copy(out=grouped[:, e], in_=pslot[:].rearrange("p t b -> p b t"))
-
-        def expert_layer(bt, grouped):
+        def quantise_slot(bt, grouped):
             scodes = codep.tile([P, E * P], U32, align_bytes=64)
             sscales = codep.tile([P, E * P], U8, align_bytes=64)
             nc.vector.quantize_mx(
@@ -172,14 +114,116 @@ def tile_softmoedynamics_pa_t_kernel(tc, tokens, logits, W1, b1, g1, be1, out):
                 scales=sscales[:],
                 in_=grouped[:].rearrange("p e b t -> p (e b t)"),
             )
+            codes[bt] = (scodes, sscales)
+
+        def unit_p():
+            u = state["p"]
+            if u >= E * len(p_tiles):
+                return
+            state["p"] = u + 1
+            bt, e = p_tiles[u // E], u % E
+            parts, on_scalar = MODES[u // E]
+            if e == 0:
+                tok = tokp.tile([P, NA, DK], BF16, tag="tok")
+                nc.sync.dma_start(out=tok[:], in_=tokens[bt * P : (bt + 1) * P])
+                grouped = grpp.tile([P, E, P, PACK], BF16, align_bytes=64, tag="grp_p")
+                live["p"] = (tok, grouped)
+            tok, grouped = live["p"]
+            prod = prodp.tile([P, parts, DK], F32, tag="prod")
+            for r in range(NA // parts):
+                for q in range(parts):
+                    n = q * (NA // parts) + r
+                    w = disp[:, bt, n, e : e + 1]
+                    if r > 0:
+                        nc.vector.scalar_tensor_tensor(
+                            out=prod[:, q, :], in0=tok[:, n, :], scalar=w, in1=prod[:, q, :],
+                            op0=ALU.mult, op1=ALU.add,
+                        )
+                    elif q < on_scalar:
+                        nc.scalar.activation(out=prod[:, q, :], in_=tok[:, n, :], func=ACT.Copy, scale=w)
+                    else:
+                        nc.vector.tensor_scalar(
+                            out=prod[:, q, :], in0=tok[:, n, :], scalar1=w, scalar2=None, op0=ALU.mult
+                        )
+            pslot = ps_slot.tile([P, PACK, P], F32, tag="pslot")
+            for t in range(PACK):
+                for q in range(parts):
+                    nc.tensor.matmul(
+                        pslot[:, t, :],
+                        lhsT=prod[:, q, t * P : (t + 1) * P],
+                        rhs=ident[:],
+                        is_transpose=True,
+                        start=(q == 0),
+                        stop=(q == parts - 1),
+                    )
+            nc.scalar.copy(out=grouped[:, e], in_=pslot[:].rearrange("p t b -> p b t"))
+            if e == E - 1:
+                quantise_slot(bt, grouped)
+
+        def unit_d():
+            u = state["d"]
+            if u >= NG * len(d_tiles):
+                return
+            state["d"] = u + 1
+            bt, g = d_tiles[u // NG], u % NG
+            if g == 0:
+                shape = [P, E, GB, NA]
+                yexp = bdp.tile(shape, F32)
+                nc.vector.tensor_tensor(
+                    out=yexp[:],
+                    in0=disp[:, bt].rearrange("p n e -> p e n").unsqueeze(2).to_broadcast(shape),
+                    in1=mask16[:].unsqueeze(1).unsqueeze(3).to_broadcast(shape),
+                    op=ALU.mult,
+                )
+                bd = bdp.tile([P, NG, E, GB], F32)
+                for half in range(2):
+                    pbd = ps_bd.tile([P, 4, P], F32)
+                    for j in range(4):
+                        nc.tensor.transpose(
+                            pbd[:, j, :], yexp[:, half * 4 + j].rearrange("p c n -> p (c n)"), ident[:]
+                        )
+                    nc.vector.tensor_copy(
+                        out=bd[:, :, half * 4 : (half + 1) * 4, :],
+                        in_=pbd[:].rearrange("p e (g c) -> p g e c", c=GB),
+                    )
+                grouped = grpp.tile([P, E, P, PACK], BF16, align_bytes=64, tag="grp_d")
+                live["d"] = (bd, grouped)
+            bd, grouped = live["d"]
+            tok = tokd.tile([P, DK], BF16)
+            rows = tokens[bt * P + g * GB : bt * P + (g + 1) * GB]
+            nc.sync.dma_start(out=tok[:], in_=rows.rearrange("b n d -> (b n) d"))
+            tokf = castp.tile([P, DK], F32)
+            nc.scalar.copy(out=tokf[:], in_=tok[:])
+            pslot = ps_slot.tile([P, PACK, P], F32, tag="pslot")
+            for t in range(PACK):
+                nc.tensor.matmul(
+                    pslot[:, t, :],
+                    lhsT=tokf[:, t * P : (t + 1) * P],
+                    rhs=bd[:, g].rearrange("p e c -> p (e c)"),
+                    start=True,
+                    stop=True,
+                )
+            nc.scalar.copy(
+                out=grouped[:, :, g * GB : (g + 1) * GB, :],
+                in_=pslot[:].rearrange("p t (e c) -> p e c t", c=GB),
+            )
+            if g == NG - 1:
+                quantise_slot(bt, grouped)
+
+        epi = {}
+
+        def stage_1(bt):
+            while bt not in codes:
+                if KINDS[bt] == "P":
+                    unit_p()
+                else:
+                    unit_d()
+            scodes, sscales = codes[bt]
             x = xp.tile([P, E, H], F32)
             tv = tvp.tile([P, E, H], F32)
-            u = up.tile([P, E * H], F32)
             sx = statp.tile([P, E], F32)
             negmu = statp.tile([P, E], F32)
             ssq = statp.tile([P, E], F32)
-            vareps = statp.tile([P, E], F32)
-            rstd = statp.tile([P, E], F32)
             for e in range(E):
                 ph = ps_h.tile([P, H], F32)
                 nc.tensor.matmul_mx(
@@ -192,59 +236,88 @@ def tile_softmoedynamics_pa_t_kernel(tc, tokens, logits, W1, b1, g1, be1, out):
                     stop=True,
                 )
                 nc.vector.scalar_tensor_tensor(
-                    out=x[:, e, :],
-                    in0=ph[:],
-                    scalar=1.0,
-                    in1=b1b[:, e * H : (e + 1) * H],
-                    op0=ALU.mult,
-                    op1=ALU.add,
-                    accum_out=sx[:, e : e + 1],
+                    out=x[:, e, :], in0=ph[:], scalar=1.0, in1=b1b[:, e * H : (e + 1) * H],
+                    op0=ALU.mult, op1=ALU.add, accum_out=sx[:, e : e + 1],
                 )
             nc.vector.tensor_scalar(out=negmu[:], in0=sx[:], scalar1=-1.0 / H, scalar2=None, op0=ALU.mult)
             for e in range(E):
                 junk = junkp.tile([P, H], BF16)
                 nc.scalar.activation(
-                    out=junk[:],
-                    in_=x[:, e, :],
-                    func=ACT.Square,
-                    bias=negmu[:, e : e + 1],
-                    scale=1.0,
+                    out=junk[:], in_=x[:, e, :], func=ACT.Square, bias=negmu[:, e : e + 1], scale=1.0,
                     accum_out=ssq[:, e : e + 1],
                 )
                 nc.vector.scalar_tensor_tensor(
-                    out=tv[:, e, :],
-                    in0=x[:, e, :],
-                    scalar=negmu[:, e : e + 1],
-                    in1=g1b[:, e * H : (e + 1) * H],
-                    op0=ALU.add,
-                    op1=ALU.mult,
+                    out=tv[:, e, :], in0=x[:, e, :], scalar=negmu[:, e : e + 1],
+                    in1=g1b[:, e * H : (e + 1) * H], op0=ALU.add, op1=ALU.mult,
                 )
+            epi[bt] = {"tv": tv, "ssq": ssq}
+
+        def stage_stats(bt):
+            vareps = statp.tile([P, E], F32)
+            rstd = statp.tile([P, E], F32)
             nc.vector.tensor_scalar(
-                out=vareps[:], in0=ssq[:], scalar1=1.0 / H, scalar2=EPS, op0=ALU.mult, op1=ALU.add
+                out=vareps[:], in0=epi[bt]["ssq"][:], scalar1=1.0 / H, scalar2=EPS, op0=ALU.mult, op1=ALU.add
             )
             nc.gpsimd.tensor_tensor(out=rstd[:], in0=vareps[:], in1=neghalf[:], op=ALU.pow)
+            epi[bt]["rstd"] = rstd
+
+        def stage_d(bt):
+            tv, rstd = epi[bt]["tv"], epi[bt]["rstd"]
             for e in range(E):
                 nc.vector.scalar_tensor_tensor(
-                    out=tv[:, e, :],
-                    in0=tv[:, e, :],
-                    scalar=rstd[:, e : e + 1],
-                    in1=be1b[:, e * H : (e + 1) * H],
-                    op0=ALU.mult,
-                    op1=ALU.add,
+                    out=tv[:, e, :], in0=tv[:, e, :], scalar=rstd[:, e : e + 1],
+                    in1=be1b[:, e * H : (e + 1) * H], op0=ALU.mult, op1=ALU.add,
                 )
-            tvf = tv[:].rearrange("p e h -> p (e h)")
-            nc.scalar.activation(out=u[:], in_=tvf, func=ACT.Exp)
-            nc.scalar.activation(out=u[:], in_=u[:], func=ACT.Ln, bias=1.0, scale=1.0)
-            nc.scalar.activation(out=u[:], in_=u[:], func=ACT.Tanh)
-            nc.vector.tensor_tensor(out=u[:], in0=tvf, in1=u[:], op=ALU.mult)
-            nc.sync.dma_start(out=out[bt * P : (bt + 1) * P].rearrange("b e h -> b (e h)"), in_=u[:])
 
-        for e in range(E):
-            quantise_w(e)
-        for bt in ORDER:
-            grouped = grpp.tile([P, E, P, PACK], BF16, align_bytes=64)
-            if bt in BD_TILES:
-                slot_block_diagonal(bt, grouped)
+        width = E * H // PIECES
+
+        def mish_piece(bt, kind, up):
+            s = epi[bt]
+            c = s.get(kind, 0)
+            s[kind] = c + 1
+            cs = slice(c * width, (c + 1) * width)
+            tvf = s["tv"][:].rearrange("p e h -> p (e h)")
+            if kind == "E":
+                if c == 0:
+                    u_new = up.tile([P, E * H], F32, tag="u")
+                    s["u"] = u_new
+                nc.scalar.activation(out=s["u"][:, cs], in_=tvf[:, cs], func=ACT.Exp)
+            elif kind == "F":
+                nc.scalar.activation(out=s["u"][:, cs], in_=s["u"][:, cs], func=ACT.Ln, bias=1.0, scale=1.0)
+            elif kind == "G":
+                nc.scalar.activation(out=s["u"][:, cs], in_=s["u"][:, cs], func=ACT.Tanh)
             else:
-                slot_products(bt, grouped)
-            expert_layer(bt, grouped)
+                nc.vector.tensor_tensor(out=s["u"][:, cs], in0=tvf[:, cs], in1=s["u"][:, cs], op=ALU.mult)
+                outf = out[bt * P : (bt + 1) * P].rearrange("b e h -> b (e h)")
+                nc.sync.dma_start(out=outf[:, cs], in_=s["u"][:, cs])
+
+        with tc.tile_pool(name="wstage", bufs=2) as wstage:
+            for tk in PROLOGUE:
+                if tk == "p":
+                    unit_p()
+                elif tk == "d":
+                    unit_d()
+                else:
+                    quantise_w(int(tk[1:]), wstage)
+        up = ctx.enter_context(tc.tile_pool(name="up", bufs=2))
+        for j in range(-1, NBT):
+            for tk in PERIOD:
+                if tk == "p":
+                    unit_p()
+                elif tk == "d":
+                    unit_d()
+                elif tk == "S1":
+                    if j + 1 < NBT:
+                        stage_1(j + 1)
+                elif tk == "ST":
+                    if j + 1 < NBT:
+                        stage_stats(j + 1)
+                elif tk == "D":
+                    if j + 1 < NBT:
+                        stage_d(j + 1)
+                elif tk == "H":
+                    if j >= 0:
+                        for c in range(PIECES):
+                            mish_piece(j, "H", up)
+                elif j >= 0:
+                    mish_piece(j, tk, up)

@@ -22,9 +22,9 @@ EPS = 1e-5
 FLOPS = 2 * B * E * DK * H + 2 * B * E * NA * DK
 
 KINDS = "DPDPDPPP"
-MODES = ((2, 2), (4, 2), (4, 2), (8, 2), (8, 2))
+MODES = ((4, 2), (8, 0), (8, 0), (8, 0), (8, 0))
 W_ON_VECTOR = (1, 3, 5, 7)
-PROLOGUE = ("W0", "d", "d", "p", "W1", "d", "d", "p", "W2", "d", "d", "p", "W3", "d", "d", "p", "W4", "p", "W5", "p", "W6", "p", "W7", "p")
+PROLOGUE = ("d", "d", "p", "W0", "d", "d", "W1", "p", "W2", "d", "d", "Lb", "W3", "p", "d", "d", "W4", "Lg", "p", "W5", "p", "W6", "Le", "p", "W7", "p", "p")
 PERIOD = ("E", "E", "S1", "p", "ST", "d", "F", "d", "F", "p", "D", "G", "d", "G", "p", "H", "p", "d", "p")
 PIECES = 2
 
@@ -34,12 +34,12 @@ def tile_softmoedynamics_pa_t_kernel(tc, tokens, logits, W1, b1, g1, be1, out):
     with ExitStack() as ctx:
         const = ctx.enter_context(tc.tile_pool(name="const", bufs=1))
         tokp = ctx.enter_context(tc.tile_pool(name="tokp", bufs=2))
-        tokd = ctx.enter_context(tc.tile_pool(name="tokd", bufs=4))
-        castp = ctx.enter_context(tc.tile_pool(name="castp", bufs=3))
+        tokd = ctx.enter_context(tc.tile_pool(name="tokd", bufs=2))
+        castp = ctx.enter_context(tc.tile_pool(name="castp", bufs=2))
         bdp = ctx.enter_context(tc.tile_pool(name="bdp", bufs=1))
-        prodp = ctx.enter_context(tc.tile_pool(name="prodp", bufs=2))
+        prodp = ctx.enter_context(tc.tile_pool(name="prodp", bufs=3))
         grpp = ctx.enter_context(tc.tile_pool(name="grpp", bufs=1))
-        codep = ctx.enter_context(tc.tile_pool(name="codep", bufs=3))
+        codep = ctx.enter_context(tc.tile_pool(name="codep", bufs=2))
         xp = ctx.enter_context(tc.tile_pool(name="xp", bufs=1))
         tvp = ctx.enter_context(tc.tile_pool(name="tvp", bufs=2))
         junkp = ctx.enter_context(tc.tile_pool(name="junkp", bufs=2))
@@ -47,9 +47,6 @@ def tile_softmoedynamics_pa_t_kernel(tc, tokens, logits, W1, b1, g1, be1, out):
         ps_bd = ctx.enter_context(tc.psum_pool(name="ps_bd", bufs=1))
         ps_slot = ctx.enter_context(tc.psum_pool(name="ps_slot", bufs=4))
         ps_h = ctx.enter_context(tc.psum_pool(name="ps_h", bufs=3))
-
-        lg = const.tile([P, NBT, NA, E], BF16)
-        nc.sync.dma_start(out=lg[:], in_=logits.rearrange("(t p) n e -> p t n e", p=P))
 
         ident = const.tile([P, P], F32)
         make_identity(nc, ident[:])
@@ -63,23 +60,9 @@ def tile_softmoedynamics_pa_t_kernel(tc, tokens, logits, W1, b1, g1, be1, out):
         b1b = const.tile([P, E * H], BF16)
         g1b = const.tile([P, E * H], BF16)
         be1b = const.tile([P, E * H], BF16)
-        nc.scalar.dma_start(out=b1b[:], in_=b1.rearrange("e h -> (e h)").partition_broadcast(P))
-        nc.scalar.dma_start(out=g1b[:], in_=g1.rearrange("e h -> (e h)").partition_broadcast(P))
-        nc.scalar.dma_start(out=be1b[:], in_=be1.rearrange("e h -> (e h)").partition_broadcast(P))
 
         full = [P, NBT, NA, E]
-        mx = const.tile([P, NBT, E], F32)
-        nc.vector.tensor_reduce(out=mx[:], in_=lg[:].rearrange("p t n e -> p t e n"), axis=AX.X, op=ALU.max)
-        ex = const.tile(full, F32)
-        nc.vector.tensor_tensor(out=ex[:], in0=lg[:], in1=mx[:].unsqueeze(2).to_broadcast(full), op=ALU.subtract)
-        exf = ex[:].rearrange("p t n e -> p (t n e)")
-        nc.scalar.activation(out=exf, in_=exf, func=ACT.Exp)
-        den = const.tile([P, NBT, E], F32)
-        nc.vector.tensor_reduce(out=den[:], in_=ex[:].rearrange("p t n e -> p t e n"), axis=AX.X, op=ALU.add)
-        rden = const.tile([P, NBT, E], F32)
-        nc.vector.reciprocal(out=rden[:], in_=den[:])
         disp = const.tile(full, F32)
-        nc.vector.tensor_tensor(out=disp[:], in0=ex[:], in1=rden[:].unsqueeze(2).to_broadcast(full), op=ALU.mult)
 
         wcodes = const.tile([P, E, H], U32, align_bytes=64)
         wscales = const.tile([P, E, H], U8, align_bytes=64)
@@ -168,7 +151,7 @@ def tile_softmoedynamics_pa_t_kernel(tc, tokens, logits, W1, b1, g1, be1, out):
             bt, g = d_tiles[u // NG], u % NG
             if g == 0:
                 shape = [P, E, GB, NA]
-                yexp = bdp.tile(shape, F32)
+                yexp = prodp.tile(shape, F32, tag="prod")
                 nc.vector.tensor_tensor(
                     out=yexp[:],
                     in0=disp[:, bt].rearrange("p n e -> p e n").unsqueeze(2).to_broadcast(shape),
@@ -291,12 +274,33 @@ def tile_softmoedynamics_pa_t_kernel(tc, tokens, logits, W1, b1, g1, be1, out):
                 outf = out[bt * P : (bt + 1) * P].rearrange("b e h -> b (e h)")
                 nc.sync.dma_start(out=outf[:, cs], in_=s["u"][:, cs])
 
-        with tc.tile_pool(name="wstage", bufs=2) as wstage:
+        with tc.tile_pool(name="early", bufs=1) as early, tc.tile_pool(name="wstage", bufs=2) as wstage:
+            lg = early.tile([P, NBT, NA, E], BF16)
+            nc.sync.dma_start(out=lg[:], in_=logits.rearrange("(t p) n e -> p t n e", p=P))
+
+            mx = early.tile([P, NBT, E], F32)
+            nc.vector.tensor_reduce(out=mx[:], in_=lg[:].rearrange("p t n e -> p t e n"), axis=AX.X, op=ALU.max)
+            ex = early.tile(full, F32)
+            nc.vector.tensor_tensor(out=ex[:], in0=lg[:], in1=mx[:].unsqueeze(2).to_broadcast(full), op=ALU.subtract)
+            exf = ex[:].rearrange("p t n e -> p (t n e)")
+            nc.scalar.activation(out=exf, in_=exf, func=ACT.Exp)
+            den = early.tile([P, NBT, E], F32)
+            nc.vector.tensor_reduce(out=den[:], in_=ex[:].rearrange("p t n e -> p t e n"), axis=AX.X, op=ALU.add)
+            rden = early.tile([P, NBT, E], F32)
+            nc.vector.reciprocal(out=rden[:], in_=den[:])
+            nc.vector.tensor_tensor(out=disp[:], in0=ex[:], in1=rden[:].unsqueeze(2).to_broadcast(full), op=ALU.mult)
+
             for tk in PROLOGUE:
                 if tk == "p":
                     unit_p()
                 elif tk == "d":
                     unit_d()
+                elif tk == "Lb":
+                    nc.sync.dma_start(out=b1b[:], in_=b1.rearrange("e h -> (e h)").partition_broadcast(P))
+                elif tk == "Lg":
+                    nc.sync.dma_start(out=g1b[:], in_=g1.rearrange("e h -> (e h)").partition_broadcast(P))
+                elif tk == "Le":
+                    nc.sync.dma_start(out=be1b[:], in_=be1.rearrange("e h -> (e h)").partition_broadcast(P))
                 else:
                     quantise_w(int(tk[1:]), wstage)
         up = ctx.enter_context(tc.tile_pool(name="up", bufs=2))

@@ -22,7 +22,7 @@ EPS = 1e-5
 FLOPS = 2 * B * E * DK * H + 2 * B * E * NA * DK
 
 KINDS = "DPDPDPPP"
-MODES = ((4, 2), (8, 0), (8, 0), (8, 0), (8, 0))
+MODES = ((4, 2), (4, 4), (8, 0), (4, 3), (8, 0))
 W_ON_VECTOR = (1, 3, 5, 7)
 PROLOGUE = ("d", "d", "p", "W0", "d", "d", "W1", "p", "W2", "d", "d", "Lb", "W3", "p", "d", "d", "W4", "Lg", "p", "W5", "p", "W6", "Le", "p", "W7", "p", "p")
 PERIOD = ("E", "E", "S1", "p", "ST", "d", "F", "d", "F", "p", "D", "G", "d", "G", "p", "H", "p", "d", "p")

@@ -25,7 +25,7 @@ KINDS = "DPDPDPPP"
 MODES = ((4, 2), (4, 4), (8, 0), (4, 3), (8, 0))
 W_ON_VECTOR = (1, 3, 5, 7)
 PROLOGUE = ("d", "d", "p", "W0", "d", "d", "W1", "p", "W2", "d", "d", "Lb", "W3", "p", "d", "d", "W4", "Lg", "p", "W5", "p", "W6", "Le", "p", "W7", "p", "p")
-PERIOD = ("E", "E", "S1", "p", "ST", "d", "F", "d", "F", "p", "D", "G", "d", "G", "p", "H", "p", "d", "p")
+PERIOD = ("E", "E", "S1", "p", "d", "F", "d", "F", "p", "D", "G", "d", "G", "p", "H", "p", "d", "p")
 PIECES = 2
 
 
@@ -44,9 +44,8 @@ def tile_softmoedynamics_pa_t_kernel(tc, tokens, logits, W1, b1, g1, be1, out):
         tvp = ctx.enter_context(tc.tile_pool(name="tvp", bufs=2))
         junkp = ctx.enter_context(tc.tile_pool(name="junkp", bufs=2))
         statp = ctx.enter_context(tc.tile_pool(name="statp", bufs=2))
-        ps_bd = ctx.enter_context(tc.psum_pool(name="ps_bd", bufs=1))
         ps_slot = ctx.enter_context(tc.psum_pool(name="ps_slot", bufs=4))
-        ps_h = ctx.enter_context(tc.psum_pool(name="ps_h", bufs=3))
+        ps_h = ctx.enter_context(tc.psum_pool(name="ps_h", bufs=4))
 
         ident = const.tile([P, P], F32)
         make_identity(nc, ident[:])
@@ -160,12 +159,12 @@ def tile_softmoedynamics_pa_t_kernel(tc, tokens, logits, W1, b1, g1, be1, out):
                 )
                 bd = bdp.tile([P, NG, E, GB], F32)
                 for half in range(2):
-                    pbd = ps_bd.tile([P, 4, P], F32)
+                    pbd = ps_slot.tile([P, 4, P], F32, tag="pslot")
                     for j in range(4):
                         nc.tensor.transpose(
                             pbd[:, j, :], yexp[:, half * 4 + j].rearrange("p c n -> p (c n)"), ident[:]
                         )
-                    nc.vector.tensor_copy(
+                    nc.scalar.copy(
                         out=bd[:, :, half * 4 : (half + 1) * 4, :],
                         in_=pbd[:].rearrange("p e (g c) -> p g e c", c=GB),
                     )
@@ -223,26 +222,25 @@ def tile_softmoedynamics_pa_t_kernel(tc, tokens, logits, W1, b1, g1, be1, out):
                     op0=ALU.mult, op1=ALU.add, accum_out=sx[:, e : e + 1],
                 )
             nc.vector.tensor_scalar(out=negmu[:], in0=sx[:], scalar1=-1.0 / H, scalar2=None, op0=ALU.mult)
-            for e in range(E):
-                junk = junkp.tile([P, H], BF16)
-                nc.scalar.activation(
-                    out=junk[:], in_=x[:, e, :], func=ACT.Square, bias=negmu[:, e : e + 1], scale=1.0,
-                    accum_out=ssq[:, e : e + 1],
-                )
-                nc.vector.scalar_tensor_tensor(
-                    out=tv[:, e, :], in0=x[:, e, :], scalar=negmu[:, e : e + 1],
-                    in1=g1b[:, e * H : (e + 1) * H], op0=ALU.add, op1=ALU.mult,
-                )
-            epi[bt] = {"tv": tv, "ssq": ssq}
-
-        def stage_stats(bt):
             vareps = statp.tile([P, E], F32)
             rstd = statp.tile([P, E], F32)
-            nc.vector.tensor_scalar(
-                out=vareps[:], in0=epi[bt]["ssq"][:], scalar1=1.0 / H, scalar2=EPS, op0=ALU.mult, op1=ALU.add
-            )
-            nc.gpsimd.tensor_tensor(out=rstd[:], in0=vareps[:], in1=neghalf[:], op=ALU.pow)
-            epi[bt]["rstd"] = rstd
+            for half in range(2):
+                hs = slice(half * (E // 2), (half + 1) * (E // 2))
+                for e in range(half * (E // 2), (half + 1) * (E // 2)):
+                    junk = junkp.tile([P, H], BF16)
+                    nc.scalar.activation(
+                        out=junk[:], in_=x[:, e, :], func=ACT.Square, bias=negmu[:, e : e + 1], scale=1.0,
+                        accum_out=ssq[:, e : e + 1],
+                    )
+                    nc.vector.scalar_tensor_tensor(
+                        out=tv[:, e, :], in0=x[:, e, :], scalar=negmu[:, e : e + 1],
+                        in1=g1b[:, e * H : (e + 1) * H], op0=ALU.add, op1=ALU.mult,
+                    )
+                nc.gpsimd.tensor_scalar(
+                    out=vareps[:, hs], in0=ssq[:, hs], scalar1=1.0 / H, scalar2=EPS, op0=ALU.mult, op1=ALU.add
+                )
+                nc.gpsimd.tensor_tensor(out=rstd[:, hs], in0=vareps[:, hs], in1=neghalf[:, hs], op=ALU.pow)
+            epi[bt] = {"tv": tv, "rstd": rstd}
 
         def stage_d(bt):
             tv, rstd = epi[bt]["tv"], epi[bt]["rstd"]
@@ -255,10 +253,15 @@ def tile_softmoedynamics_pa_t_kernel(tc, tokens, logits, W1, b1, g1, be1, out):
         width = E * H // PIECES
 
         def mish_piece(bt, kind, up):
+            subs = 2 if bt == NBT - 1 else 1
+            for i in range(subs):
+                mish_part(bt, kind, up, width // subs)
+
+        def mish_part(bt, kind, up, w):
             s = epi[bt]
             c = s.get(kind, 0)
             s[kind] = c + 1
-            cs = slice(c * width, (c + 1) * width)
+            cs = slice(c * w, (c + 1) * w)
             tvf = s["tv"][:].rearrange("p e h -> p (e h)")
             if kind == "E":
                 if c == 0:
@@ -313,9 +316,6 @@ def tile_softmoedynamics_pa_t_kernel(tc, tokens, logits, W1, b1, g1, be1, out):
                 elif tk == "S1":
                     if j + 1 < NBT:
                         stage_1(j + 1)
-                elif tk == "ST":
-                    if j + 1 < NBT:
-                        stage_stats(j + 1)
                 elif tk == "D":
                     if j + 1 < NBT:
                         stage_d(j + 1)

@@ -25,7 +25,7 @@ KINDS = "DPDPDPPP"
 MODES = ((4, 2), (4, 4), (8, 0), (4, 3), (8, 0))
 W_ON_VECTOR = (1, 3, 5, 7)
 PROLOGUE = ("d", "d", "p", "W0", "d", "d", "W1", "p", "W2", "d", "d", "Lb", "W3", "p", "d", "d", "W4", "Lg", "p", "W5", "p", "W6", "Le", "p", "W7", "p", "p")
-PERIOD = ("E", "E", "S1", "p", "d", "F", "d", "F", "p", "D", "G", "d", "G", "p", "H", "p", "d", "p")
+PERIOD = ("E", "E", "S1", "p", "d", "F", "d", "F", "LV", "EV", "p", "D", "G", "d", "G", "p", "H", "p", "d", "p")
 PIECES = 2
 
 
@@ -53,8 +53,6 @@ def tile_softmoedynamics_pa_t_kernel(tc, tokens, logits, W1, b1, g1, be1, out):
         nc.vector.tensor_reduce(
             out=mask16[:], in_=ident[:].rearrange("p (g c) -> p c g", c=GB), axis=AX.X, op=ALU.add
         )
-        neghalf = const.tile([P, E], F32)
-        nc.vector.memset(neghalf[:], -0.5)
 
         b1b = const.tile([P, E * H], BF16)
         g1b = const.tile([P, E * H], BF16)
@@ -222,25 +220,27 @@ def tile_softmoedynamics_pa_t_kernel(tc, tokens, logits, W1, b1, g1, be1, out):
                     op0=ALU.mult, op1=ALU.add, accum_out=sx[:, e : e + 1],
                 )
             nc.vector.tensor_scalar(out=negmu[:], in0=sx[:], scalar1=-1.0 / H, scalar2=None, op0=ALU.mult)
-            vareps = statp.tile([P, E], F32)
-            rstd = statp.tile([P, E], F32)
-            for half in range(2):
-                hs = slice(half * (E // 2), (half + 1) * (E // 2))
-                for e in range(half * (E // 2), (half + 1) * (E // 2)):
-                    junk = junkp.tile([P, H], BF16)
-                    nc.scalar.activation(
-                        out=junk[:], in_=x[:, e, :], func=ACT.Square, bias=negmu[:, e : e + 1], scale=1.0,
-                        accum_out=ssq[:, e : e + 1],
-                    )
-                    nc.vector.scalar_tensor_tensor(
-                        out=tv[:, e, :], in0=x[:, e, :], scalar=negmu[:, e : e + 1],
-                        in1=g1b[:, e * H : (e + 1) * H], op0=ALU.add, op1=ALU.mult,
-                    )
-                nc.gpsimd.tensor_scalar(
-                    out=vareps[:, hs], in0=ssq[:, hs], scalar1=1.0 / H, scalar2=EPS, op0=ALU.mult, op1=ALU.add
+            for e in range(E):
+                junk = junkp.tile([P, H], BF16)
+                nc.scalar.activation(
+                    out=junk[:], in_=x[:, e, :], func=ACT.Square, bias=negmu[:, e : e + 1], scale=1.0,
+                    accum_out=ssq[:, e : e + 1],
                 )
-                nc.gpsimd.tensor_tensor(out=rstd[:, hs], in0=vareps[:, hs], in1=neghalf[:, hs], op=ALU.pow)
-            epi[bt] = {"tv": tv, "rstd": rstd}
+                nc.vector.scalar_tensor_tensor(
+                    out=tv[:, e, :], in0=x[:, e, :], scalar=negmu[:, e : e + 1],
+                    in1=g1b[:, e * H : (e + 1) * H], op0=ALU.add, op1=ALU.mult,
+                )
+            epi[bt] = {"tv": tv, "ssq": ssq}
+
+        def stage_ln_var(bt):
+            lnvar = statp.tile([P, E], F32)
+            nc.scalar.activation(out=lnvar[:], in_=epi[bt]["ssq"][:], func=ACT.Ln, bias=EPS, scale=1.0 / H)
+            epi[bt]["lnvar"] = lnvar
+
+        def stage_rstd(bt):
+            rstd = statp.tile([P, E], F32)
+            nc.scalar.activation(out=rstd[:], in_=epi[bt]["lnvar"][:], func=ACT.Exp, scale=-0.5)
+            epi[bt]["rstd"] = rstd
 
         def stage_d(bt):
             tv, rstd = epi[bt]["tv"], epi[bt]["rstd"]
@@ -316,6 +316,12 @@ def tile_softmoedynamics_pa_t_kernel(tc, tokens, logits, W1, b1, g1, be1, out):
                 elif tk == "S1":
                     if j + 1 < NBT:
                         stage_1(j + 1)
+                elif tk == "LV":
+                    if j + 1 < NBT:
+                        stage_ln_var(j + 1)
+                elif tk == "EV":
+                    if j + 1 < NBT:
+                        stage_rstd(j + 1)
                 elif tk == "D":
                     if j + 1 < NBT:
                         stage_d(j + 1)

@@ -13,321 +13,303 @@ ACT = mybir.ActivationFunctionType
 AX = mybir.AxisListType
 
 P = 128
-B, NA, E, DK, H = 1024, 8, 8, 512, 512
-NBT = B // P
+B, AGENTS, E, K, H = 1024, 8, 8, 512, 512
+TILES = B // P
 PACK = 4
-GB = 16
-NG = P // GB
+GROUP = P // AGENTS
+GROUPS = P // GROUP
 EPS = 1e-5
-FLOPS = 2 * B * E * DK * H + 2 * B * E * NA * DK
+FLOPS = 2 * B * E * K * H + 2 * B * E * AGENTS * K
 
-KINDS = "DPDPDPPP"
-MODES = ((4, 2), (4, 4), (8, 0), (4, 3), (8, 0))
-W_ON_VECTOR = (1, 3, 5, 7)
-PROLOGUE = ("d", "d", "p", "W0", "d", "d", "W1", "p", "W2", "d", "d", "Lb", "W3", "p", "d", "d", "W4", "Lg", "p", "W5", "p", "W6", "Le", "p", "W7", "p", "p")
-PERIOD = ("E", "E", "S1", "p", "d", "F", "d", "F", "LV", "EV", "p", "D", "G", "d", "G", "p", "H", "p", "d", "p")
-PIECES = 2
+BLOCK_TILES = (0, 2, 4)
+PARTS = 4
+ON_SCALAR = 2
+HALVES = (slice(0, E * H // 2), slice(E * H // 2, E * H))
 
 
 def tile_softmoedynamics_pa_t_kernel(tc, tokens, logits, W1, b1, g1, be1, out):
     nc = tc.nc
     with ExitStack() as ctx:
         const = ctx.enter_context(tc.tile_pool(name="const", bufs=1))
-        tokp = ctx.enter_context(tc.tile_pool(name="tokp", bufs=2))
-        tokd = ctx.enter_context(tc.tile_pool(name="tokd", bufs=2))
-        castp = ctx.enter_context(tc.tile_pool(name="castp", bufs=2))
-        bdp = ctx.enter_context(tc.tile_pool(name="bdp", bufs=1))
-        prodp = ctx.enter_context(tc.tile_pool(name="prodp", bufs=3))
-        grpp = ctx.enter_context(tc.tile_pool(name="grpp", bufs=1))
-        codep = ctx.enter_context(tc.tile_pool(name="codep", bufs=2))
-        xp = ctx.enter_context(tc.tile_pool(name="xp", bufs=1))
-        tvp = ctx.enter_context(tc.tile_pool(name="tvp", bufs=2))
-        junkp = ctx.enter_context(tc.tile_pool(name="junkp", bufs=2))
-        statp = ctx.enter_context(tc.tile_pool(name="statp", bufs=2))
-        ps_slot = ctx.enter_context(tc.psum_pool(name="ps_slot", bufs=4))
-        ps_h = ctx.enter_context(tc.psum_pool(name="ps_h", bufs=4))
+        tok_pool = ctx.enter_context(tc.tile_pool(name="tok_pool", bufs=2))
+        group_pool = ctx.enter_context(tc.tile_pool(name="group_pool", bufs=2))
+        diag_pool = ctx.enter_context(tc.tile_pool(name="diag_pool", bufs=1))
+        sum_pool = ctx.enter_context(tc.tile_pool(name="sum_pool", bufs=3))
+        slot_pool = ctx.enter_context(tc.tile_pool(name="slot_pool", bufs=1))
+        code_pool = ctx.enter_context(tc.tile_pool(name="code_pool", bufs=2))
+        x_pool = ctx.enter_context(tc.tile_pool(name="x_pool", bufs=1))
+        v_pool = ctx.enter_context(tc.tile_pool(name="v_pool", bufs=2))
+        small = ctx.enter_context(tc.tile_pool(name="small", bufs=2))
+        slot_banks = ctx.enter_context(tc.psum_pool(name="slot_banks", bufs=4))
+        layer_banks = ctx.enter_context(tc.psum_pool(name="layer_banks", bufs=4))
 
-        ident = const.tile([P, P], F32)
-        make_identity(nc, ident[:])
-        mask16 = const.tile([P, GB], F32)
+        identity = const.tile([P, P], F32)
+        make_identity(nc, identity[:])
+        same_batch = const.tile([P, GROUP], F32)
         nc.vector.tensor_reduce(
-            out=mask16[:], in_=ident[:].rearrange("p (g c) -> p c g", c=GB), axis=AX.X, op=ALU.add
+            out=same_batch[:], in_=identity[:].rearrange("p (g c) -> p c g", c=GROUP), axis=AX.X, op=ALU.add
         )
+        minus_half = const.tile([P, E], F32)
+        nc.vector.memset(minus_half[:], -0.5)
 
-        b1b = const.tile([P, E * H], BF16)
-        g1b = const.tile([P, E * H], BF16)
-        be1b = const.tile([P, E * H], BF16)
+        bias_rows = const.tile([P, E * H], BF16)
+        gain_rows = const.tile([P, E * H], BF16)
+        shift_rows = const.tile([P, E * H], BF16)
+        disp = const.tile([P, TILES, AGENTS, E], F32)
+        w_codes = const.tile([P, E, H], U32, align_bytes=64)
+        w_scales = const.tile([P, E, H], U8, align_bytes=64)
 
-        full = [P, NBT, NA, E]
-        disp = const.tile(full, F32)
+        def softmax_over_agents(pool):
+            shape = [P, TILES, AGENTS, E]
+            raw = pool.tile(shape, BF16)
+            nc.sync.dma_start(out=raw[:], in_=logits.rearrange("(t p) n e -> p t n e", p=P))
+            top = pool.tile([P, TILES, E], F32)
+            nc.vector.tensor_reduce(out=top[:], in_=raw[:].rearrange("p t n e -> p t e n"), axis=AX.X, op=ALU.max)
+            ex = pool.tile(shape, F32)
+            nc.vector.tensor_tensor(out=ex[:], in0=raw[:], in1=top[:].unsqueeze(2).to_broadcast(shape), op=ALU.subtract)
+            flat = ex[:].rearrange("p t n e -> p (t n e)")
+            nc.scalar.activation(out=flat, in_=flat, func=ACT.Exp)
+            total = pool.tile([P, TILES, E], F32)
+            nc.vector.tensor_reduce(out=total[:], in_=ex[:].rearrange("p t n e -> p t e n"), axis=AX.X, op=ALU.add)
+            inverse = pool.tile([P, TILES, E], F32)
+            nc.vector.reciprocal(out=inverse[:], in_=total[:])
+            nc.vector.tensor_tensor(
+                out=disp[:], in0=ex[:], in1=inverse[:].unsqueeze(2).to_broadcast(shape), op=ALU.mult
+            )
 
-        wcodes = const.tile([P, E, H], U32, align_bytes=64)
-        wscales = const.tile([P, E, H], U8, align_bytes=64)
-
-        def quantise_w(e, wstage):
-            wraw = wstage.tile([P, PACK, H], BF16)
-            nc.sync.dma_start(out=wraw[:], in_=W1[e].rearrange("(t p) h -> p t h", p=P))
-            wgrp = wstage.tile([P, H, PACK], BF16, align_bytes=64)
-            dst = wgrp[:].rearrange("p (c i) t -> p c t i", i=4)
-            src = wraw[:].rearrange("p t (c i) -> p c t i", i=4)
-            if e in W_ON_VECTOR:
+        def quantise_weights(e, pool):
+            rows = pool.tile([P, PACK, H], BF16)
+            nc.sync.dma_start(out=rows[:], in_=W1[e].rearrange("(t p) h -> p t h", p=P))
+            words = pool.tile([P, H, PACK], BF16, align_bytes=64)
+            dst = words[:].rearrange("p (c i) t -> p c t i", i=4)
+            src = rows[:].rearrange("p t (c i) -> p c t i", i=4)
+            if e % 2 == 1:
                 nc.vector.tensor_copy(out=dst, in_=src)
             else:
                 nc.scalar.copy(out=dst, in_=src)
             nc.vector.quantize_mx(
-                out=wcodes[:, e, :].bitcast(FP8X4),
-                scales=wscales[:, e, :],
-                in_=wgrp[:].rearrange("p h t -> p (h t)"),
+                out=w_codes[:, e, :].bitcast(FP8X4),
+                scales=w_scales[:, e, :],
+                in_=words[:].rearrange("p h t -> p (h t)"),
             )
 
-        p_tiles = [bt for bt in range(NBT) if KINDS[bt] == "P"]
-        d_tiles = [bt for bt in range(NBT) if KINDS[bt] == "D"]
-        state = {"p": 0, "d": 0}
-        live = {}
-        codes = {}
+        product_tiles = [bt for bt in range(TILES) if bt not in BLOCK_TILES]
+        made = {"product": 0, "block": 0}
+        current = {}
+        slot_codes = {}
 
-        def quantise_slot(bt, grouped):
-            scodes = codep.tile([P, E * P], U32, align_bytes=64)
-            sscales = codep.tile([P, E * P], U8, align_bytes=64)
+        def quantise_slots(bt, words):
+            codes = code_pool.tile([P, E * P], U32, align_bytes=64)
+            scales = code_pool.tile([P, E * P], U8, align_bytes=64)
             nc.vector.quantize_mx(
-                out=scodes[:].bitcast(FP8X4),
-                scales=sscales[:],
-                in_=grouped[:].rearrange("p e b t -> p (e b t)"),
+                out=codes[:].bitcast(FP8X4), scales=scales[:], in_=words[:].rearrange("p e b t -> p (e b t)")
             )
-            codes[bt] = (scodes, sscales)
+            slot_codes[bt] = (codes, scales)
 
-        def unit_p():
-            u = state["p"]
-            if u >= E * len(p_tiles):
+        def product_unit():
+            unit = made["product"]
+            if unit == E * len(product_tiles):
                 return
-            state["p"] = u + 1
-            bt, e = p_tiles[u // E], u % E
-            parts, on_scalar = MODES[u // E]
+            made["product"] = unit + 1
+            bt, e = product_tiles[unit // E], unit % E
             if e == 0:
-                tok = tokp.tile([P, NA, DK], BF16, tag="tok")
+                tok = tok_pool.tile([P, AGENTS, K], BF16)
                 nc.sync.dma_start(out=tok[:], in_=tokens[bt * P : (bt + 1) * P])
-                grouped = grpp.tile([P, E, P, PACK], BF16, align_bytes=64, tag="grp_p")
-                live["p"] = (tok, grouped)
-            tok, grouped = live["p"]
-            prod = prodp.tile([P, parts, DK], F32, tag="prod")
-            for r in range(NA // parts):
+                words = slot_pool.tile([P, E, P, PACK], BF16, align_bytes=64, tag="product_words")
+                current["product"] = (tok, words)
+            tok, words = current["product"]
+            parts, on_scalar = PARTS, ON_SCALAR
+            sums = sum_pool.tile([P, parts, K], F32, tag="sums")
+            length = AGENTS // parts
+            for r in range(length):
                 for q in range(parts):
-                    n = q * (NA // parts) + r
-                    w = disp[:, bt, n, e : e + 1]
+                    n = q * length + r
+                    weight = disp[:, bt, n, e : e + 1]
                     if r > 0:
                         nc.vector.scalar_tensor_tensor(
-                            out=prod[:, q, :], in0=tok[:, n, :], scalar=w, in1=prod[:, q, :],
+                            out=sums[:, q, :], in0=tok[:, n, :], scalar=weight, in1=sums[:, q, :],
                             op0=ALU.mult, op1=ALU.add,
                         )
                     elif q < on_scalar:
-                        nc.scalar.activation(out=prod[:, q, :], in_=tok[:, n, :], func=ACT.Copy, scale=w)
+                        nc.scalar.activation(out=sums[:, q, :], in_=tok[:, n, :], func=ACT.Copy, scale=weight)
                     else:
                         nc.vector.tensor_scalar(
-                            out=prod[:, q, :], in0=tok[:, n, :], scalar1=w, scalar2=None, op0=ALU.mult
+                            out=sums[:, q, :], in0=tok[:, n, :], scalar1=weight, scalar2=None, op0=ALU.mult
                         )
-            pslot = ps_slot.tile([P, PACK, P], F32, tag="pslot")
+            bank = slot_banks.tile([P, PACK, P], F32, tag="bank")
             for t in range(PACK):
                 for q in range(parts):
                     nc.tensor.matmul(
-                        pslot[:, t, :],
-                        lhsT=prod[:, q, t * P : (t + 1) * P],
-                        rhs=ident[:],
-                        is_transpose=True,
-                        start=(q == 0),
-                        stop=(q == parts - 1),
+                        bank[:, t, :], lhsT=sums[:, q, t * P : (t + 1) * P], rhs=identity[:],
+                        is_transpose=True, start=(q == 0), stop=(q == parts - 1),
                     )
-            nc.scalar.copy(out=grouped[:, e], in_=pslot[:].rearrange("p t b -> p b t"))
+            nc.scalar.copy(out=words[:, e], in_=bank[:].rearrange("p t b -> p b t"))
             if e == E - 1:
-                quantise_slot(bt, grouped)
+                quantise_slots(bt, words)
 
-        def unit_d():
-            u = state["d"]
-            if u >= NG * len(d_tiles):
+        def block_unit():
+            unit = made["block"]
+            if unit == GROUPS * len(BLOCK_TILES):
                 return
-            state["d"] = u + 1
-            bt, g = d_tiles[u // NG], u % NG
+            made["block"] = unit + 1
+            bt, g = BLOCK_TILES[unit // GROUPS], unit % GROUPS
             if g == 0:
-                shape = [P, E, GB, NA]
-                yexp = prodp.tile(shape, F32, tag="prod")
+                shape = [P, E, GROUP, AGENTS]
+                spread = sum_pool.tile(shape, F32, tag="sums")
                 nc.vector.tensor_tensor(
-                    out=yexp[:],
+                    out=spread[:],
                     in0=disp[:, bt].rearrange("p n e -> p e n").unsqueeze(2).to_broadcast(shape),
-                    in1=mask16[:].unsqueeze(1).unsqueeze(3).to_broadcast(shape),
+                    in1=same_batch[:].unsqueeze(1).unsqueeze(3).to_broadcast(shape),
                     op=ALU.mult,
                 )
-                bd = bdp.tile([P, NG, E, GB], F32)
+                diag = diag_pool.tile([P, GROUPS, E, GROUP], F32)
                 for half in range(2):
-                    pbd = ps_slot.tile([P, 4, P], F32, tag="pslot")
-                    for j in range(4):
+                    bank = slot_banks.tile([P, PACK, P], F32, tag="bank")
+                    for i in range(PACK):
                         nc.tensor.transpose(
-                            pbd[:, j, :], yexp[:, half * 4 + j].rearrange("p c n -> p (c n)"), ident[:]
+                            bank[:, i, :], spread[:, half * PACK + i].rearrange("p c n -> p (c n)"), identity[:]
                         )
                     nc.scalar.copy(
-                        out=bd[:, :, half * 4 : (half + 1) * 4, :],
-                        in_=pbd[:].rearrange("p e (g c) -> p g e c", c=GB),
+                        out=diag[:, :, half * PACK : (half + 1) * PACK, :],
+                        in_=bank[:].rearrange("p e (g c) -> p g e c", c=GROUP),
                     )
-                grouped = grpp.tile([P, E, P, PACK], BF16, align_bytes=64, tag="grp_d")
-                live["d"] = (bd, grouped)
-            bd, grouped = live["d"]
-            tok = tokd.tile([P, DK], BF16)
-            rows = tokens[bt * P + g * GB : bt * P + (g + 1) * GB]
-            nc.sync.dma_start(out=tok[:], in_=rows.rearrange("b n d -> (b n) d"))
-            tokf = castp.tile([P, DK], F32)
-            nc.scalar.copy(out=tokf[:], in_=tok[:])
-            pslot = ps_slot.tile([P, PACK, P], F32, tag="pslot")
+                words = slot_pool.tile([P, E, P, PACK], BF16, align_bytes=64, tag="block_words")
+                current["block"] = (diag, words)
+            diag, words = current["block"]
+            tok = group_pool.tile([P, K], BF16)
+            first = bt * P + g * GROUP
+            nc.sync.dma_start(out=tok[:], in_=tokens[first : first + GROUP].rearrange("b n k -> (b n) k"))
+            tok32 = group_pool.tile([P, K], F32)
+            nc.scalar.copy(out=tok32[:], in_=tok[:])
+            bank = slot_banks.tile([P, PACK, P], F32, tag="bank")
             for t in range(PACK):
                 nc.tensor.matmul(
-                    pslot[:, t, :],
-                    lhsT=tokf[:, t * P : (t + 1) * P],
-                    rhs=bd[:, g].rearrange("p e c -> p (e c)"),
-                    start=True,
-                    stop=True,
+                    bank[:, t, :], lhsT=tok32[:, t * P : (t + 1) * P], rhs=diag[:, g].rearrange("p e c -> p (e c)"),
+                    start=True, stop=True,
                 )
             nc.scalar.copy(
-                out=grouped[:, :, g * GB : (g + 1) * GB, :],
-                in_=pslot[:].rearrange("p t (e c) -> p e c t", c=GB),
+                out=words[:, :, g * GROUP : (g + 1) * GROUP, :],
+                in_=bank[:].rearrange("p t (e c) -> p e c t", c=GROUP),
             )
-            if g == NG - 1:
-                quantise_slot(bt, grouped)
+            if g == GROUPS - 1:
+                quantise_slots(bt, words)
 
-        epi = {}
+        work = {}
 
-        def stage_1(bt):
-            while bt not in codes:
-                if KINDS[bt] == "P":
-                    unit_p()
-                else:
-                    unit_d()
-            scodes, sscales = codes[bt]
-            x = xp.tile([P, E, H], F32)
-            tv = tvp.tile([P, E, H], F32)
-            sx = statp.tile([P, E], F32)
-            negmu = statp.tile([P, E], F32)
-            ssq = statp.tile([P, E], F32)
+        def layer_and_centre(bt):
+            if bt == TILES:
+                return
+            codes, scales = slot_codes[bt]
+            x = x_pool.tile([P, E, H], F32)
+            v = v_pool.tile([P, E, H], F32)
+            total = small.tile([P, E], F32)
+            minus_mean = small.tile([P, E], F32)
+            squares = small.tile([P, E], F32)
             for e in range(E):
-                ph = ps_h.tile([P, H], F32)
+                bank = layer_banks.tile([P, H], F32)
                 nc.tensor.matmul_mx(
-                    out=ph[:],
-                    lhsT=scodes[:, e * P : (e + 1) * P].bitcast(FP8X4),
-                    lhsT_scale=sscales[:, e * P : (e + 1) * P],
-                    rhs=wcodes[:, e, :].bitcast(FP8X4),
-                    rhs_scale=wscales[:, e, :],
+                    out=bank[:],
+                    lhsT=codes[:, e * P : (e + 1) * P].bitcast(FP8X4),
+                    lhsT_scale=scales[:, e * P : (e + 1) * P],
+                    rhs=w_codes[:, e, :].bitcast(FP8X4),
+                    rhs_scale=w_scales[:, e, :],
                     start=True,
                     stop=True,
                 )
                 nc.vector.scalar_tensor_tensor(
-                    out=x[:, e, :], in0=ph[:], scalar=1.0, in1=b1b[:, e * H : (e + 1) * H],
-                    op0=ALU.mult, op1=ALU.add, accum_out=sx[:, e : e + 1],
+                    out=x[:, e, :], in0=bank[:], scalar=1.0, in1=bias_rows[:, e * H : (e + 1) * H],
+                    op0=ALU.mult, op1=ALU.add, accum_out=total[:, e : e + 1],
                 )
-            nc.vector.tensor_scalar(out=negmu[:], in0=sx[:], scalar1=-1.0 / H, scalar2=None, op0=ALU.mult)
+            nc.vector.tensor_scalar(out=minus_mean[:], in0=total[:], scalar1=-1.0 / H, scalar2=None, op0=ALU.mult)
             for e in range(E):
-                junk = junkp.tile([P, H], BF16)
+                unused = small.tile([P, H], BF16)
                 nc.scalar.activation(
-                    out=junk[:], in_=x[:, e, :], func=ACT.Square, bias=negmu[:, e : e + 1], scale=1.0,
-                    accum_out=ssq[:, e : e + 1],
+                    out=unused[:], in_=x[:, e, :], func=ACT.Square, bias=minus_mean[:, e : e + 1], scale=1.0,
+                    accum_out=squares[:, e : e + 1],
                 )
                 nc.vector.scalar_tensor_tensor(
-                    out=tv[:, e, :], in0=x[:, e, :], scalar=negmu[:, e : e + 1],
-                    in1=g1b[:, e * H : (e + 1) * H], op0=ALU.add, op1=ALU.mult,
+                    out=v[:, e, :], in0=x[:, e, :], scalar=minus_mean[:, e : e + 1],
+                    in1=gain_rows[:, e * H : (e + 1) * H], op0=ALU.add, op1=ALU.mult,
                 )
-            epi[bt] = {"tv": tv, "ssq": ssq}
+            work[bt] = {"v": v, "squares": squares}
 
-        def stage_ln_var(bt):
-            lnvar = statp.tile([P, E], F32)
-            nc.scalar.activation(out=lnvar[:], in_=epi[bt]["ssq"][:], func=ACT.Ln, bias=EPS, scale=1.0 / H)
-            epi[bt]["lnvar"] = lnvar
+        def inverse_std(bt):
+            if bt == TILES:
+                return
+            variance = small.tile([P, E], F32)
+            inverse = small.tile([P, E], F32)
+            nc.vector.tensor_scalar(
+                out=variance[:], in0=work[bt]["squares"][:], scalar1=1.0 / H, scalar2=EPS, op0=ALU.mult, op1=ALU.add
+            )
+            nc.gpsimd.tensor_tensor(out=inverse[:], in0=variance[:], in1=minus_half[:], op=ALU.pow)
+            work[bt]["inverse"] = inverse
 
-        def stage_rstd(bt):
-            rstd = statp.tile([P, E], F32)
-            nc.scalar.activation(out=rstd[:], in_=epi[bt]["lnvar"][:], func=ACT.Exp, scale=-0.5)
-            epi[bt]["rstd"] = rstd
-
-        def stage_d(bt):
-            tv, rstd = epi[bt]["tv"], epi[bt]["rstd"]
+        def scale_and_shift(bt):
+            if bt == TILES:
+                return
+            v, inverse = work[bt]["v"], work[bt]["inverse"]
             for e in range(E):
                 nc.vector.scalar_tensor_tensor(
-                    out=tv[:, e, :], in0=tv[:, e, :], scalar=rstd[:, e : e + 1],
-                    in1=be1b[:, e * H : (e + 1) * H], op0=ALU.mult, op1=ALU.add,
+                    out=v[:, e, :], in0=v[:, e, :], scalar=inverse[:, e : e + 1],
+                    in1=shift_rows[:, e * H : (e + 1) * H], op0=ALU.mult, op1=ALU.add,
                 )
 
-        width = E * H // PIECES
+        def mish_exp(bt, pool):
+            if bt < 0:
+                return
+            u = pool.tile([P, E * H], F32)
+            work[bt]["u"] = u
+            v = work[bt]["v"][:].rearrange("p e h -> p (e h)")
+            for cols in HALVES:
+                nc.scalar.activation(out=u[:, cols], in_=v[:, cols], func=ACT.Exp)
 
-        def mish_piece(bt, kind, up):
-            subs = 2 if bt == NBT - 1 else 1
-            for i in range(subs):
-                mish_part(bt, kind, up, width // subs)
+        def mish_log(bt):
+            if bt < 0:
+                return
+            u = work[bt]["u"]
+            for cols in HALVES:
+                nc.scalar.activation(out=u[:, cols], in_=u[:, cols], func=ACT.Ln, bias=1.0, scale=1.0)
 
-        def mish_part(bt, kind, up, w):
-            s = epi[bt]
-            c = s.get(kind, 0)
-            s[kind] = c + 1
-            cs = slice(c * w, (c + 1) * w)
-            tvf = s["tv"][:].rearrange("p e h -> p (e h)")
-            if kind == "E":
-                if c == 0:
-                    u_new = up.tile([P, E * H], F32, tag="u")
-                    s["u"] = u_new
-                nc.scalar.activation(out=s["u"][:, cs], in_=tvf[:, cs], func=ACT.Exp)
-            elif kind == "F":
-                nc.scalar.activation(out=s["u"][:, cs], in_=s["u"][:, cs], func=ACT.Ln, bias=1.0, scale=1.0)
-            elif kind == "G":
-                nc.scalar.activation(out=s["u"][:, cs], in_=s["u"][:, cs], func=ACT.Tanh)
-            else:
-                nc.vector.tensor_tensor(out=s["u"][:, cs], in0=tvf[:, cs], in1=s["u"][:, cs], op=ALU.mult)
-                outf = out[bt * P : (bt + 1) * P].rearrange("b e h -> b (e h)")
-                nc.sync.dma_start(out=outf[:, cs], in_=s["u"][:, cs])
+        def mish_tanh(bt):
+            if bt < 0:
+                return
+            u = work[bt]["u"]
+            for cols in HALVES:
+                nc.scalar.activation(out=u[:, cols], in_=u[:, cols], func=ACT.Tanh)
 
-        with tc.tile_pool(name="early", bufs=1) as early, tc.tile_pool(name="wstage", bufs=2) as wstage:
-            lg = early.tile([P, NBT, NA, E], BF16)
-            nc.sync.dma_start(out=lg[:], in_=logits.rearrange("(t p) n e -> p t n e", p=P))
+        def multiply_and_store(bt):
+            if bt < 0:
+                return
+            u = work[bt]["u"]
+            v = work[bt]["v"][:].rearrange("p e h -> p (e h)")
+            rows = out[bt * P : (bt + 1) * P].rearrange("b e h -> b (e h)")
+            for cols in HALVES:
+                nc.vector.tensor_tensor(out=u[:, cols], in0=v[:, cols], in1=u[:, cols], op=ALU.mult)
+                nc.sync.dma_start(out=rows[:, cols], in_=u[:, cols])
 
-            mx = early.tile([P, NBT, E], F32)
-            nc.vector.tensor_reduce(out=mx[:], in_=lg[:].rearrange("p t n e -> p t e n"), axis=AX.X, op=ALU.max)
-            ex = early.tile(full, F32)
-            nc.vector.tensor_tensor(out=ex[:], in0=lg[:], in1=mx[:].unsqueeze(2).to_broadcast(full), op=ALU.subtract)
-            exf = ex[:].rearrange("p t n e -> p (t n e)")
-            nc.scalar.activation(out=exf, in_=exf, func=ACT.Exp)
-            den = early.tile([P, NBT, E], F32)
-            nc.vector.tensor_reduce(out=den[:], in_=ex[:].rearrange("p t n e -> p t e n"), axis=AX.X, op=ALU.add)
-            rden = early.tile([P, NBT, E], F32)
-            nc.vector.reciprocal(out=rden[:], in_=den[:])
-            nc.vector.tensor_tensor(out=disp[:], in0=ex[:], in1=rden[:].unsqueeze(2).to_broadcast(full), op=ALU.mult)
-
-            for tk in PROLOGUE:
-                if tk == "p":
-                    unit_p()
-                elif tk == "d":
-                    unit_d()
-                elif tk == "Lb":
-                    nc.sync.dma_start(out=b1b[:], in_=b1.rearrange("e h -> (e h)").partition_broadcast(P))
-                elif tk == "Lg":
-                    nc.sync.dma_start(out=g1b[:], in_=g1.rearrange("e h -> (e h)").partition_broadcast(P))
-                elif tk == "Le":
-                    nc.sync.dma_start(out=be1b[:], in_=be1.rearrange("e h -> (e h)").partition_broadcast(P))
-                else:
-                    quantise_w(int(tk[1:]), wstage)
-        up = ctx.enter_context(tc.tile_pool(name="up", bufs=2))
-        for j in range(-1, NBT):
-            for tk in PERIOD:
-                if tk == "p":
-                    unit_p()
-                elif tk == "d":
-                    unit_d()
-                elif tk == "S1":
-                    if j + 1 < NBT:
-                        stage_1(j + 1)
-                elif tk == "LV":
-                    if j + 1 < NBT:
-                        stage_ln_var(j + 1)
-                elif tk == "EV":
-                    if j + 1 < NBT:
-                        stage_rstd(j + 1)
-                elif tk == "D":
-                    if j + 1 < NBT:
-                        stage_d(j + 1)
-                elif tk == "H":
-                    if j >= 0:
-                        for c in range(PIECES):
-                            mish_piece(j, "H", up)
-                elif j >= 0:
-                    mish_piece(j, tk, up)
+        with tc.tile_pool(name="early", bufs=1) as early, tc.tile_pool(name="staging", bufs=2) as staging:
+            softmax_over_agents(early)
+            for e in range(E):
+                block_unit()
+                product_unit()
+                quantise_weights(e, staging)
+            for rows, vector in ((bias_rows, b1), (gain_rows, g1), (shift_rows, be1)):
+                nc.sync.dma_start(out=rows[:], in_=vector.rearrange("e h -> (e h)").partition_broadcast(P))
+        mish_pool = ctx.enter_context(tc.tile_pool(name="mish_pool", bufs=2))
+        for j in range(-1, TILES):
+            mish_exp(j, mish_pool)
+            layer_and_centre(j + 1)
+            product_unit()
+            inverse_std(j + 1)
+            block_unit()
+            mish_log(j)
+            product_unit()
+            block_unit()
+            scale_and_shift(j + 1)
+            mish_tanh(j)
+            product_unit()
+            block_unit()
+            multiply_and_store(j)
+            product_unit()
+            block_unit()
+            product_unit()

from contextlib import ExitStack

import concourse.mybir as mybir
from concourse.masks import make_identity

F32 = mybir.dt.float32
BF16 = mybir.dt.bfloat16
U32 = mybir.dt.uint32
U8 = mybir.dt.uint8
FP8X4 = mybir.dt.float8_e4m3fn_x4
ALU = mybir.AluOpType
ACT = mybir.ActivationFunctionType
AX = mybir.AxisListType

P = 128
B, AGENTS, E, K, H = 1024, 8, 8, 512, 512
TILES = B // P
PACK = 4
GROUP = P // AGENTS
GROUPS = P // GROUP
EPS = 1e-5
FLOPS = 2 * B * E * K * H + 2 * B * E * AGENTS * K

BLOCK_TILES = (0, 2, 4)
PARTS = 4
ON_SCALAR = 2
HALVES = (slice(0, E * H // 2), slice(E * H // 2, E * H))


def tile_softmoedynamics_pa_t_kernel(tc, tokens, logits, W1, b1, g1, be1, out):
    nc = tc.nc
    with ExitStack() as ctx:
        const = ctx.enter_context(tc.tile_pool(name="const", bufs=1))
        tok_pool = ctx.enter_context(tc.tile_pool(name="tok_pool", bufs=2))
        group_pool = ctx.enter_context(tc.tile_pool(name="group_pool", bufs=2))
        diag_pool = ctx.enter_context(tc.tile_pool(name="diag_pool", bufs=1))
        sum_pool = ctx.enter_context(tc.tile_pool(name="sum_pool", bufs=3))
        slot_pool = ctx.enter_context(tc.tile_pool(name="slot_pool", bufs=1))
        code_pool = ctx.enter_context(tc.tile_pool(name="code_pool", bufs=2))
        x_pool = ctx.enter_context(tc.tile_pool(name="x_pool", bufs=1))
        v_pool = ctx.enter_context(tc.tile_pool(name="v_pool", bufs=2))
        small = ctx.enter_context(tc.tile_pool(name="small", bufs=2))
        slot_banks = ctx.enter_context(tc.psum_pool(name="slot_banks", bufs=4))
        layer_banks = ctx.enter_context(tc.psum_pool(name="layer_banks", bufs=4))

        identity = const.tile([P, P], F32)
        make_identity(nc, identity[:])
        same_batch = const.tile([P, GROUP], F32)
        nc.vector.tensor_reduce(
            out=same_batch[:], in_=identity[:].rearrange("p (g c) -> p c g", c=GROUP), axis=AX.X, op=ALU.add
        )
        minus_half = const.tile([P, E], F32)
        nc.vector.memset(minus_half[:], -0.5)

        bias_rows = const.tile([P, E * H], BF16)
        gain_rows = const.tile([P, E * H], BF16)
        shift_rows = const.tile([P, E * H], BF16)
        disp = const.tile([P, TILES, AGENTS, E], F32)
        w_codes = const.tile([P, E, H], U32, align_bytes=64)
        w_scales = const.tile([P, E, H], U8, align_bytes=64)

        def softmax_over_agents(pool):
            shape = [P, TILES, AGENTS, E]
            raw = pool.tile(shape, BF16)
            nc.sync.dma_start(out=raw[:], in_=logits.rearrange("(t p) n e -> p t n e", p=P))
            top = pool.tile([P, TILES, E], F32)
            nc.vector.tensor_reduce(out=top[:], in_=raw[:].rearrange("p t n e -> p t e n"), axis=AX.X, op=ALU.max)
            ex = pool.tile(shape, F32)
            nc.vector.tensor_tensor(out=ex[:], in0=raw[:], in1=top[:].unsqueeze(2).to_broadcast(shape), op=ALU.subtract)
            flat = ex[:].rearrange("p t n e -> p (t n e)")
            nc.scalar.activation(out=flat, in_=flat, func=ACT.Exp)
            total = pool.tile([P, TILES, E], F32)
            nc.vector.tensor_reduce(out=total[:], in_=ex[:].rearrange("p t n e -> p t e n"), axis=AX.X, op=ALU.add)
            inverse = pool.tile([P, TILES, E], F32)
            nc.vector.reciprocal(out=inverse[:], in_=total[:])
            nc.vector.tensor_tensor(
                out=disp[:], in0=ex[:], in1=inverse[:].unsqueeze(2).to_broadcast(shape), op=ALU.mult
            )

        def quantise_weights(e, pool):
            rows = pool.tile([P, PACK, H], BF16)
            nc.sync.dma_start(out=rows[:], in_=W1[e].rearrange("(t p) h -> p t h", p=P))
            words = pool.tile([P, H, PACK], BF16, align_bytes=64)
            dst = words[:].rearrange("p (c i) t -> p c t i", i=4)
            src = rows[:].rearrange("p t (c i) -> p c t i", i=4)
            if e % 2 == 1:
                nc.vector.tensor_copy(out=dst, in_=src)
            else:
                nc.scalar.copy(out=dst, in_=src)
            nc.vector.quantize_mx(
                out=w_codes[:, e, :].bitcast(FP8X4),
                scales=w_scales[:, e, :],
                in_=words[:].rearrange("p h t -> p (h t)"),
            )

        product_tiles = [bt for bt in range(TILES) if bt not in BLOCK_TILES]
        made = {"product": 0, "block": 0}
        current = {}
        slot_codes = {}

        def quantise_slots(bt, words):
            codes = code_pool.tile([P, E * P], U32, align_bytes=64)
            scales = code_pool.tile([P, E * P], U8, align_bytes=64)
            nc.vector.quantize_mx(
                out=codes[:].bitcast(FP8X4), scales=scales[:], in_=words[:].rearrange("p e b t -> p (e b t)")
            )
            slot_codes[bt] = (codes, scales)

        def product_unit():
            unit = made["product"]
            if unit == E * len(product_tiles):
                return
            made["product"] = unit + 1
            bt, e = product_tiles[unit // E], unit % E
            if e == 0:
                tok = tok_pool.tile([P, AGENTS, K], BF16)
                nc.sync.dma_start(out=tok[:], in_=tokens[bt * P : (bt + 1) * P])
                words = slot_pool.tile([P, E, P, PACK], BF16, align_bytes=64, tag="product_words")
                current["product"] = (tok, words)
            tok, words = current["product"]
            parts, on_scalar = PARTS, ON_SCALAR
            sums = sum_pool.tile([P, parts, K], F32, tag="sums")
            length = AGENTS // parts
            for r in range(length):
                for q in range(parts):
                    n = q * length + r
                    weight = disp[:, bt, n, e : e + 1]
                    if r > 0:
                        nc.vector.scalar_tensor_tensor(
                            out=sums[:, q, :], in0=tok[:, n, :], scalar=weight, in1=sums[:, q, :],
                            op0=ALU.mult, op1=ALU.add,
                        )
                    elif q < on_scalar:
                        nc.scalar.activation(out=sums[:, q, :], in_=tok[:, n, :], func=ACT.Copy, scale=weight)
                    else:
                        nc.vector.tensor_scalar(
                            out=sums[:, q, :], in0=tok[:, n, :], scalar1=weight, scalar2=None, op0=ALU.mult
                        )
            bank = slot_banks.tile([P, PACK, P], F32, tag="bank")
            for t in range(PACK):
                for q in range(parts):
                    nc.tensor.matmul(
                        bank[:, t, :], lhsT=sums[:, q, t * P : (t + 1) * P], rhs=identity[:],
                        is_transpose=True, start=(q == 0), stop=(q == parts - 1),
                    )
            nc.scalar.copy(out=words[:, e], in_=bank[:].rearrange("p t b -> p b t"))
            if e == E - 1:
                quantise_slots(bt, words)

        def block_unit():
            unit = made["block"]
            if unit == GROUPS * len(BLOCK_TILES):
                return
            made["block"] = unit + 1
            bt, g = BLOCK_TILES[unit // GROUPS], unit % GROUPS
            if g == 0:
                shape = [P, E, GROUP, AGENTS]
                spread = sum_pool.tile(shape, F32, tag="sums")
                nc.vector.tensor_tensor(
                    out=spread[:],
                    in0=disp[:, bt].rearrange("p n e -> p e n").unsqueeze(2).to_broadcast(shape),
                    in1=same_batch[:].unsqueeze(1).unsqueeze(3).to_broadcast(shape),
                    op=ALU.mult,
                )
                diag = diag_pool.tile([P, GROUPS, E, GROUP], F32)
                for half in range(2):
                    bank = slot_banks.tile([P, PACK, P], F32, tag="bank")
                    for i in range(PACK):
                        nc.tensor.transpose(
                            bank[:, i, :], spread[:, half * PACK + i].rearrange("p c n -> p (c n)"), identity[:]
                        )
                    nc.scalar.copy(
                        out=diag[:, :, half * PACK : (half + 1) * PACK, :],
                        in_=bank[:].rearrange("p e (g c) -> p g e c", c=GROUP),
                    )
                words = slot_pool.tile([P, E, P, PACK], BF16, align_bytes=64, tag="block_words")
                current["block"] = (diag, words)
            diag, words = current["block"]
            tok = group_pool.tile([P, K], BF16)
            first = bt * P + g * GROUP
            nc.sync.dma_start(out=tok[:], in_=tokens[first : first + GROUP].rearrange("b n k -> (b n) k"))
            tok32 = group_pool.tile([P, K], F32)
            nc.scalar.copy(out=tok32[:], in_=tok[:])
            bank = slot_banks.tile([P, PACK, P], F32, tag="bank")
            for t in range(PACK):
                nc.tensor.matmul(
                    bank[:, t, :], lhsT=tok32[:, t * P : (t + 1) * P], rhs=diag[:, g].rearrange("p e c -> p (e c)"),
                    start=True, stop=True,
                )
            nc.scalar.copy(
                out=words[:, :, g * GROUP : (g + 1) * GROUP, :],
                in_=bank[:].rearrange("p t (e c) -> p e c t", c=GROUP),
            )
            if g == GROUPS - 1:
                quantise_slots(bt, words)

        work = {}

        def layer_and_centre(bt):
            if bt == TILES:
                return
            codes, scales = slot_codes[bt]
            x = x_pool.tile([P, E, H], F32)
            v = v_pool.tile([P, E, H], F32)
            total = small.tile([P, E], F32)
            minus_mean = small.tile([P, E], F32)
            squares = small.tile([P, E], F32)
            for e in range(E):
                bank = layer_banks.tile([P, H], F32)
                nc.tensor.matmul_mx(
                    out=bank[:],
                    lhsT=codes[:, e * P : (e + 1) * P].bitcast(FP8X4),
                    lhsT_scale=scales[:, e * P : (e + 1) * P],
                    rhs=w_codes[:, e, :].bitcast(FP8X4),
                    rhs_scale=w_scales[:, e, :],
                    start=True,
                    stop=True,
                )
                nc.vector.scalar_tensor_tensor(
                    out=x[:, e, :], in0=bank[:], scalar=1.0, in1=bias_rows[:, e * H : (e + 1) * H],
                    op0=ALU.mult, op1=ALU.add, accum_out=total[:, e : e + 1],
                )
            nc.vector.tensor_scalar(out=minus_mean[:], in0=total[:], scalar1=-1.0 / H, scalar2=None, op0=ALU.mult)
            for e in range(E):
                unused = small.tile([P, H], BF16)
                nc.scalar.activation(
                    out=unused[:], in_=x[:, e, :], func=ACT.Square, bias=minus_mean[:, e : e + 1], scale=1.0,
                    accum_out=squares[:, e : e + 1],
                )
                nc.vector.scalar_tensor_tensor(
                    out=v[:, e, :], in0=x[:, e, :], scalar=minus_mean[:, e : e + 1],
                    in1=gain_rows[:, e * H : (e + 1) * H], op0=ALU.add, op1=ALU.mult,
                )
            work[bt] = {"v": v, "squares": squares}

        def inverse_std(bt):
            if bt == TILES:
                return
            variance = small.tile([P, E], F32)
            inverse = small.tile([P, E], F32)
            nc.vector.tensor_scalar(
                out=variance[:], in0=work[bt]["squares"][:], scalar1=1.0 / H, scalar2=EPS, op0=ALU.mult, op1=ALU.add
            )
            nc.gpsimd.tensor_tensor(out=inverse[:], in0=variance[:], in1=minus_half[:], op=ALU.pow)
            work[bt]["inverse"] = inverse

        def scale_and_shift(bt):
            if bt == TILES:
                return
            v, inverse = work[bt]["v"], work[bt]["inverse"]
            for e in range(E):
                nc.vector.scalar_tensor_tensor(
                    out=v[:, e, :], in0=v[:, e, :], scalar=inverse[:, e : e + 1],
                    in1=shift_rows[:, e * H : (e + 1) * H], op0=ALU.mult, op1=ALU.add,
                )

        def mish_exp(bt, pool):
            if bt < 0:
                return
            u = pool.tile([P, E * H], F32)
            work[bt]["u"] = u
            v = work[bt]["v"][:].rearrange("p e h -> p (e h)")
            for cols in HALVES:
                nc.scalar.activation(out=u[:, cols], in_=v[:, cols], func=ACT.Exp)

        def mish_log(bt):
            if bt < 0:
                return
            u = work[bt]["u"]
            for cols in HALVES:
                nc.scalar.activation(out=u[:, cols], in_=u[:, cols], func=ACT.Ln, bias=1.0, scale=1.0)

        def mish_tanh(bt):
            if bt < 0:
                return
            u = work[bt]["u"]
            for cols in HALVES:
                nc.scalar.activation(out=u[:, cols], in_=u[:, cols], func=ACT.Tanh)

        def multiply_and_store(bt):
            if bt < 0:
                return
            u = work[bt]["u"]
            v = work[bt]["v"][:].rearrange("p e h -> p (e h)")
            rows = out[bt * P : (bt + 1) * P].rearrange("b e h -> b (e h)")
            for cols in HALVES:
                nc.vector.tensor_tensor(out=u[:, cols], in0=v[:, cols], in1=u[:, cols], op=ALU.mult)
                nc.sync.dma_start(out=rows[:, cols], in_=u[:, cols])

        with tc.tile_pool(name="early", bufs=1) as early, tc.tile_pool(name="staging", bufs=2) as staging:
            softmax_over_agents(early)
            for e in range(E):
                block_unit()
                product_unit()
                quantise_weights(e, staging)
            for rows, vector in ((bias_rows, b1), (gain_rows, g1), (shift_rows, be1)):
                nc.sync.dma_start(out=rows[:], in_=vector.rearrange("e h -> (e h)").partition_broadcast(P))
        mish_pool = ctx.enter_context(tc.tile_pool(name="mish_pool", bufs=2))
        for j in range(-1, TILES):
            mish_exp(j, mish_pool)
            layer_and_centre(j + 1)
            product_unit()
            inverse_std(j + 1)
            block_unit()
            mish_log(j)
            product_unit()
            block_unit()
            scale_and_shift(j + 1)
            mish_tanh(j)
            product_unit()
            block_unit()
            multiply_and_store(j)
            product_unit()
            block_unit()
            product_unit()
